import numpy as np
import ml_dtypes


def mxq(x, axis, fmt="e4m3"):
    dtype, down = {"e4m3": (ml_dtypes.float8_e4m3fn, 7), "e5m2": (ml_dtypes.float8_e5m2, 14)}[fmt]
    v = np.moveaxis(np.asarray(x, np.float32).astype(ml_dtypes.bfloat16).astype(np.float64), axis, -1)
    blocks = v.reshape(v.shape[:-1] + (-1, 32))
    amax = np.abs(blocks).max(-1, keepdims=True)
    byte = np.maximum(np.where(amax > 0, np.frexp(amax)[1] - 1 + 127, 0) - down, 1)
    scale = np.exp2(byte - 127.0)
    codes = (blocks / scale).astype(np.float32).astype(dtype).astype(np.float64)
    return np.moveaxis((codes * scale).reshape(v.shape), -1, axis)


WIDE = False


def mx_kscale(k):
    if not WIDE:
        return np.ones(k)
    levels = np.array([10, -10, 5, -5, 0])
    a = np.random.permutation(np.resize(levels, k // 512 * 4)).reshape(k // 512, 4)
    idx = np.arange(k)
    return np.exp2(a[idx // 512, idx % 128 // 32])


BF16 = ml_dtypes.bfloat16


def bf(x):
    return np.asarray(x, np.float32).astype(BF16)


def f64(x):
    return np.asarray(x).astype(np.float64)


E2M1 = np.array([0.0, 0.5, 1.0, 1.5, 2.0, 3.0, 4.0, 6.0, -0.0, -0.5, -1.0, -1.5, -2.0, -3.0, -4.0, -6.0])


def pack_weight(w, fmt):
    k, n = w.shape
    w = f64(bf(w)).reshape(k // 32, 32, n)
    amax = np.abs(w).max(1)
    if fmt == "e4m3":
        byte = np.frexp(amax)[1] - 1 + 127 - 7
    else:
        mant, ex = np.frexp(amax / 6.0)
        byte = np.where(mant > 0.5, ex, ex - 1) + 127
    byte = np.clip(np.where(amax > 0, byte, 1), 1, 254)
    scaled = (w * np.exp2(127.0 - byte)[:, None, :]).reshape(k, n).astype(np.float32)
    by_word = np.ascontiguousarray(scaled.reshape(k // 512, 128, 4, n).transpose(0, 1, 3, 2))
    if fmt == "e4m3":
        words = by_word.astype(ml_dtypes.float8_e4m3fn).view(np.uint8)
    else:
        c = by_word.astype(ml_dtypes.float4_e2m1fn).view(np.uint8) & 0xF
        words = c[..., 0::2] | (c[..., 1::2] << 4)
    return np.ascontiguousarray(words), np.ascontiguousarray(byte.astype(np.uint8).reshape(k // 512, 16, n))


def unpack_weight(words, scales, fmt):
    g, p, n, _ = words.shape
    if fmt == "e4m3":
        vals = np.ascontiguousarray(words).view(ml_dtypes.float8_e4m3fn).astype(np.float64)
    else:
        nib = np.empty((g, p, n, 4), np.uint8)
        nib[..., 0::2] = words & 0xF
        nib[..., 1::2] = words >> 4
        vals = E2M1[nib]
    vals = vals * np.repeat(np.exp2(scales.astype(np.float64) - 127.0), 8, axis=1)[..., None]
    return vals.transpose(0, 1, 3, 2).reshape(g * 512, n)


N, MUL0, MUL1, MUL2, DIM1, DIM2 = 128, 4608, 384, 128, 3, 5
D_S = MUL0
D_V = MUL1 * DIM1
D_T = MUL2 * DIM2
N_GATES = MUL1 + MUL2


def sigmoid(v):
    return 1.0 / (1.0 + np.exp(-v))


def leaky_relu(v):
    return np.where(v >= 0.0, v, 0.01 * v)


def setup_inputs():
    k = mx_kscale(MUL0)
    x = np.random.standard_normal((N, D_S + D_V + D_T))
    x[:, :D_S] = x[:, :D_S] * k
    W0_words, W0_scales = pack_weight(np.random.standard_normal((MUL0, MUL0 + N_GATES)) / k[:, None], "e4m3")
    return {"x": bf(x), "W0_words": W0_words, "W0_scales": W0_scales,
            "W1": bf(np.random.standard_normal((MUL1, MUL1))), "W2": bf(np.random.standard_normal((MUL2, MUL2)))}


def reference(x, W0_words, W0_scales, W1, W2):
    x = f64(x)
    n = x.shape[0]
    s = x[:, :D_S]
    v = x[:, D_S:D_S + D_V].reshape(n, MUL1, DIM1)
    t = x[:, D_S + D_V:].reshape(n, MUL2, DIM2)
    s_out = (mxq(s, 1, "e4m3") @ unpack_weight(W0_words, W0_scales, "e4m3")) / np.sqrt(MUL0)
    v_out = (v.transpose(0, 2, 1) @ f64(W1)).transpose(0, 2, 1) / np.sqrt(MUL1)
    t_out = (t.transpose(0, 2, 1) @ f64(W2)).transpose(0, 2, 1) / np.sqrt(MUL2)
    scalars = leaky_relu(s_out[:, :MUL0])
    gates = sigmoid(s_out[:, MUL0:])
    gv = v_out * gates[:, :MUL1, None]
    gt = t_out * gates[:, MUL1:, None]
    return np.concatenate([scalars, gv.reshape(n, -1), gt.reshape(n, -1)], axis=-1)

@@ -1,0 +1,241 @@
+from contextlib import ExitStack
+import math
+
+import concourse.mybir as mybir
+from concourse.masks import make_identity
+
+F32 = mybir.dt.float32
+BF16 = mybir.dt.bfloat16
+I32 = mybir.dt.int32
+U32 = mybir.dt.uint32
+U8 = mybir.dt.uint8
+FP8X4 = mybir.dt.float8_e4m3fn_x4
+ACT = mybir.ActivationFunctionType
+ALU = mybir.AluOpType
+
+P = 128
+MUL0, MUL1, MUL2, DIM1, DIM2 = 4608, 384, 128, 3, 5
+N_OUT0 = MUL0 + MUL1 + MUL2
+GROUPS = MUL0 // 512
+V0 = MUL0
+T0 = MUL0 + MUL1 * DIM1
+D_ALL = T0 + MUL2 * DIM2
+BANK = 512
+R1_COL0 = 1024
+R1_BANKS = 8
+R2_BANKS = 2
+W_BUFS = 6
+
+INV0 = 1.0 / math.sqrt(MUL0)
+INV1 = 1.0 / math.sqrt(MUL1)
+INV2 = 1.0 / math.sqrt(MUL2)
+
+FLOPS = 2 * P * MUL0 * N_OUT0 + 2 * P * (DIM1 * MUL1 * MUL1 + DIM2 * MUL2 * MUL2)
+
+
+def tile_equivariantmlpblock_w_kernel(tc, x, W0_words, W0_scales, W1, W2, out):
+    nc = tc.nc
+    w32 = W0_words.rearrange("g p n t -> g p (n t)").bitcast(I32)
+    s32 = W0_scales.bitcast(I32)
+
+    with ExitStack() as ctx:
+        ctx.enter_context(tc.manual_schedule())
+        keep = ctx.enter_context(tc.tile_pool(name="keep", bufs=1))
+        wpool = ctx.enter_context(tc.tile_pool(name="wstream", bufs=W_BUFS))
+        psum = ctx.enter_context(tc.psum_pool(name="psum", bufs=1))
+
+        def bank_tile(shape, dtype, bank, name):
+            return psum.tile(shape, dtype, name=name, tag="bank%d" % bank)
+
+        x_sb = keep.tile([P, D_ALL], BF16, name="x_sb", align_bytes=64)
+        planes = keep.tile([P, 2 * N_OUT0 + N_OUT0 // 2], U8, name="planes", align_bytes=64)
+        ident32 = keep.tile([P, P], F32, name="ident32")
+        ident16 = keep.tile([P, P], BF16, name="ident16")
+        w1_sb = keep.tile([P, 3, MUL1], BF16, name="w1_sb")
+        w2_sb = keep.tile([P, MUL2], BF16, name="w2_sb")
+        grouped = keep.tile([P, GROUPS * 512], BF16, name="grouped", align_bytes=64)
+        x_codes = keep.tile([P, GROUPS * P], U32, name="x_codes", align_bytes=64)
+        x_scales = keep.tile([P, GROUPS * P], U8, name="x_scales", align_bytes=64)
+        vt_sb = keep.tile([P, 14, P], BF16, name="vt_sb")
+        out_sb = keep.tile([P, D_ALL], F32, name="out_sb")
+        gates = keep.tile([P, BANK], F32, name="gates")
+        warm = keep.tile([P, 1], F32, name="warm")
+        w_r2 = [
+            keep.tile([P, n, R2_BANKS * BANK], U32, name="w_r2_%d" % i, align_bytes=64)
+            for i, n in enumerate((3, 3, 2, 1))
+        ]
+        r2_first = (0, 3, 6, 8)
+
+        nc.vector.memset(planes[:].bitcast(I32), 0)
+        make_identity(nc, ident32[:])
+        make_identity(nc, ident16[:])
+        nc.scalar.activation(out=warm[:], in_=ident32[:, 0:1], func=ACT.Sigmoid)
+
+        nc.sync.dma_start(out=x_sb[:], in_=x)
+        p32 = planes[:].bitcast(I32)
+        for slot in range(2):
+            for q in range(4):
+                nc.sync.dma_start(
+                    out=p32[32 * q : 32 * q + 16, 1280 * slot : 1280 * (slot + 1)],
+                    in_=s32[4 * slot : 4 * slot + 4, 4 * q : 4 * q + 4, :],
+                )
+        for q in range(4):
+            nc.sync.dma_start(
+                out=p32[32 * q : 32 * q + 8, 2560:3200],
+                in_=s32[8, 4 * q : 4 * q + 4, :].rearrange("r (h c) -> h r c", h=2),
+            )
+        nc.sync.dma_start(out=w1_sb[:], in_=W1.rearrange("(c p) o -> p c o", p=P))
+        nc.sync.dma_start(out=w2_sb[:], in_=W2)
+
+        def load_round1(g):
+            w = wpool.tile([P, R1_BANKS * BANK], U32, name="w_r1", tag="w_r1", align_bytes=64)
+            nc.sync.dma_start(out=w[:].bitcast(I32), in_=w32[g, :, R1_COL0:N_OUT0])
+            return w
+
+        w_r1 = [load_round1(g) for g in range(W_BUFS)]
+
+        def w_scale(g, col):
+            if g < 8:
+                k = 4 * (g % 4)
+                base = N_OUT0 * (g // 4) + col
+            else:
+                h = col // (N_OUT0 // 2)
+                k = 4 * h
+                base = 2 * N_OUT0 + col - h * (N_OUT0 // 2)
+            return planes[k:P, base : base + BANK]
+
+        x32 = x_sb[:, 0:MUL0].bitcast(F32)
+        g32 = grouped[:].bitcast(F32)
+        s_ps = [bank_tile([P, 4, P], F32, i, "s_ps%d" % i) for i in range(5)]
+        for g in range(GROUPS):
+            for u in range(2):
+                nc.tensor.transpose(
+                    s_ps[g // 2][:, 2 * (g % 2) + u, :],
+                    x32[:, 256 * g + u : 256 * (g + 1) : 2],
+                    ident32[:],
+                )
+
+        def regroup(i, on_vector):
+            ng = 2 if i < 4 else 1
+            src = s_ps[i][:, 0 : 2 * ng, :].rearrange("p (g u) r -> p g r u", u=2)
+            dst = g32[:, 512 * i : 512 * i + 256 * ng].rearrange("p (g r u) -> p g r u", g=ng, u=2)
+            if on_vector:
+                nc.vector.tensor_copy(out=dst, in_=src)
+            else:
+                nc.scalar.copy(out=dst, in_=src)
+
+        def quantise(i):
+            ng = 2 if i < 4 else 1
+            nc.vector.quantize_mx(
+                out=x_codes[:, 256 * i : 256 * i + P * ng].bitcast(FP8X4),
+                scales=x_scales[:, 256 * i : 256 * i + P * ng],
+                in_=grouped[:, 1024 * i : 1024 * i + 512 * ng],
+            )
+
+        regroup(0, True)
+        regroup(1, False)
+        regroup(2, True)
+        regroup(3, False)
+        quantise(0)
+        regroup(4, True)
+        quantise(1)
+        quantise(2)
+        quantise(3)
+        quantise(4)
+
+        vt_ps = [bank_tile([P, 8, P], BF16, 5 + i, "vt_ps%d" % i) for i in range(2)]
+        vt_src = [
+            x_sb[:, V0 + 384 * c + m : V0 + 384 * (c + 1) : DIM1] for c in range(3) for m in range(DIM1)
+        ] + [x_sb[:, T0 + m : D_ALL : DIM2] for m in range(DIM2)]
+        for i, src in enumerate(vt_src):
+            nc.tensor.transpose(vt_ps[i // 7][:, i % 7, :], src, ident16[:])
+        nc.scalar.copy(out=vt_sb[:, 0:7, :], in_=vt_ps[0][:, 0:7, :])
+        nc.vector.tensor_copy(out=vt_sb[:, 7:14, :], in_=vt_ps[1][:, 0:7, :])
+
+        for oc in range(3):
+            v_ps = bank_tile([P, DIM1, P], F32, (7, 0, 1)[oc], "v_ps%d" % oc)
+            for m in range(DIM1):
+                for c in range(3):
+                    nc.tensor.matmul(
+                        out=v_ps[:, m, :],
+                        lhsT=vt_sb[:, 3 * c + m, :],
+                        rhs=w1_sb[:, c, P * oc : P * (oc + 1)],
+                        start=(c == 0),
+                        stop=(c == 2),
+                    )
+            dst = out_sb[:, V0 + 384 * oc : V0 + 384 * (oc + 1)].rearrange("p (o m) -> p o m", m=DIM1)
+            src = v_ps[:].rearrange("p m o -> p o m")
+            if oc == 1:
+                nc.vector.tensor_scalar(out=dst, in0=src, scalar1=INV1, scalar2=None, op0=ALU.mult)
+            else:
+                nc.scalar.activation(out=dst, in_=src, func=ACT.Copy, scale=INV1)
+        for oh in range(2):
+            t_ps = bank_tile([P, DIM2, 64], F32, (2, 3)[oh], "t_ps%d" % oh)
+            for m in range(DIM2):
+                nc.tensor.matmul(
+                    out=t_ps[:, m, :],
+                    lhsT=vt_sb[:, 9 + m, :],
+                    rhs=w2_sb[:, 64 * oh : 64 * (oh + 1)],
+                    start=True,
+                    stop=True,
+                )
+            dst = out_sb[:, T0 + 320 * oh : T0 + 320 * (oh + 1)].rearrange("p (o m) -> p o m", m=DIM2)
+            src = t_ps[:].rearrange("p m o -> p o m")
+            if oh == 0:
+                nc.vector.tensor_scalar(out=dst, in0=src, scalar1=INV2, scalar2=None, op0=ALU.mult)
+            else:
+                nc.scalar.activation(out=dst, in_=src, func=ACT.Copy, scale=INV2)
+
+        def mx_pass(acc, g, words, col):
+            nc.tensor.matmul_mx(
+                out=acc[:],
+                lhsT=x_codes[:, P * g : P * (g + 1)].bitcast(FP8X4),
+                lhsT_scale=x_scales[:, P * g : P * (g + 1)],
+                rhs=words.bitcast(FP8X4),
+                rhs_scale=w_scale(g, col),
+                start=(g == 0),
+                stop=(g == GROUPS - 1),
+            )
+
+        def leaky(acc, col):
+            dst = out_sb[:, col : col + BANK]
+            nc.scalar.activation(out=dst, in_=acc[:], func=ACT.Copy, scale=INV0)
+            nc.vector.scalar_tensor_tensor(out=dst, in0=dst, scalar=0.01, in1=dst, op0=ALU.mult, op1=ALU.max)
+
+        acc1 = [bank_tile([P, BANK], F32, (4 + b) % 8, "acc1_%d" % b) for b in range(R1_BANKS)]
+        for g in range(GROUPS):
+            for b in range(R1_BANKS):
+                mx_pass(acc1[b], g, w_r1[g][:, BANK * b : BANK * (b + 1)], R1_COL0 + BANK * b)
+            if g + W_BUFS < GROUPS:
+                w_r1.append(load_round1(g + W_BUFS))
+            if g + W_BUFS == GROUPS - 1:
+                for i, tile_r2 in enumerate(w_r2):
+                    g0 = r2_first[i]
+                    n = tile_r2.shape[1]
+                    nc.sync.dma_start(
+                        out=tile_r2[:].bitcast(I32),
+                        in_=w32[g0 : g0 + n, :, 0:R1_COL0].rearrange("g p w -> p g w"),
+                    )
+
+        for b in range(R1_BANKS - 1):
+            leaky(acc1[b], R1_COL0 + BANK * b)
+        nc.scalar.activation(out=gates[:], in_=acc1[R1_BANKS - 1][:], func=ACT.Sigmoid, scale=INV0)
+        gv = out_sb[:, V0:T0].rearrange("p (o m) -> p o m", m=DIM1)
+        nc.vector.tensor_tensor(
+            out=gv, in0=gv, in1=gates[:, 0:MUL1].unsqueeze(2).to_broadcast([P, MUL1, DIM1]), op=ALU.mult
+        )
+        gt = out_sb[:, T0:D_ALL].rearrange("p (o m) -> p o m", m=DIM2)
+        nc.vector.tensor_tensor(
+            out=gt, in0=gt, in1=gates[:, MUL1:BANK].unsqueeze(2).to_broadcast([P, MUL2, DIM2]), op=ALU.mult
+        )
+
+        acc2 = [bank_tile([P, BANK], F32, (4 + b) % 8, "acc2_%d" % b) for b in range(R2_BANKS)]
+        for i, tile_r2 in enumerate(w_r2):
+            for j in range(tile_r2.shape[1]):
+                for b in range(R2_BANKS):
+                    mx_pass(acc2[b], r2_first[i] + j, tile_r2[:, j, BANK * b : BANK * (b + 1)], BANK * b)
+        for b in range(R2_BANKS):
+            leaky(acc2[b], BANK * b)
+
+        for lo, hi in ((1024, 2560), (2560, V0), (V0, D_ALL), (0, 1024)):
+            nc.sync.dma_start(out=out[:, lo:hi], in_=out_sb[:, lo:hi])

@@ -36,7 +36,7 @@ FLOPS = 2 * P * MUL0 * N_OUT0 + 2 * P * (DIM1 * MUL1 * MUL1 + DIM2 * MUL2 * MUL2
 def tile_equivariantmlpblock_w_kernel(tc, x, W0_words, W0_scales, W1, W2, out):
     nc = tc.nc
     w32 = W0_words.rearrange("g p n t -> g p (n t)").bitcast(I32)
-    s32 = W0_scales.bitcast(I32)
+    s32 = W0_scales.bitcast(F32)
 
     with ExitStack() as ctx:
         ctx.enter_context(tc.manual_schedule())
@@ -66,24 +66,31 @@ def tile_equivariantmlpblock_w_kernel(tc, x, W0_words, W0_scales, W1, W2, out):
         ]
         r2_first = (0, 3, 6, 8)
 
-        nc.vector.memset(planes[:].bitcast(I32), 0)
+        p32 = planes[:].bitcast(F32)
+        for slot in range(3):
+            nc.vector.memset(planes[:, N_OUT0 * slot : min(N_OUT0 * (slot + 1), planes.shape[1])].bitcast(I32), 0)
+
+        def load_scales(slot):
+            for q in range(4):
+                if slot < 2:
+                    nc.gpsimd.dma_start(
+                        out=p32[32 * q : 32 * q + 16, 1280 * slot : 1280 * (slot + 1)],
+                        in_=s32[4 * slot : 4 * slot + 4, 4 * q : 4 * q + 4, :],
+                    )
+                else:
+                    nc.gpsimd.dma_start(
+                        out=p32[32 * q : 32 * q + 8, 2560:3200],
+                        in_=s32[8, 4 * q : 4 * q + 4, :].rearrange("r (h c) -> h r c", h=2),
+                    )
+
         make_identity(nc, ident32[:])
+        load_scales(0)
         make_identity(nc, ident16[:])
+        load_scales(1)
+        load_scales(2)
         nc.scalar.activation(out=warm[:], in_=ident32[:, 0:1], func=ACT.Sigmoid)
 
         nc.sync.dma_start(out=x_sb[:], in_=x)
-        p32 = planes[:].bitcast(I32)
-        for slot in range(2):
-            for q in range(4):
-                nc.sync.dma_start(
-                    out=p32[32 * q : 32 * q + 16, 1280 * slot : 1280 * (slot + 1)],
-                    in_=s32[4 * slot : 4 * slot + 4, 4 * q : 4 * q + 4, :],
-                )
-        for q in range(4):
-            nc.sync.dma_start(
-                out=p32[32 * q : 32 * q + 8, 2560:3200],
-                in_=s32[8, 4 * q : 4 * q + 4, :].rearrange("r (h c) -> h r c", h=2),
-            )
         nc.sync.dma_start(out=w1_sb[:], in_=W1.rearrange("(c p) o -> p c o", p=P))
         nc.sync.dma_start(out=w2_sb[:], in_=W2)
 

@@ -70,24 +70,20 @@ def tile_equivariantmlpblock_w_kernel(tc, x, W0_words, W0_scales, W1, W2, out):
         for slot in range(3):
             nc.vector.memset(planes[:, N_OUT0 * slot : min(N_OUT0 * (slot + 1), planes.shape[1])].bitcast(I32), 0)
 
-        def load_scales(slot):
-            for q in range(4):
-                if slot < 2:
-                    nc.gpsimd.dma_start(
-                        out=p32[32 * q : 32 * q + 16, 1280 * slot : 1280 * (slot + 1)],
-                        in_=s32[4 * slot : 4 * slot + 4, 4 * q : 4 * q + 4, :],
-                    )
-                else:
-                    nc.gpsimd.dma_start(
-                        out=p32[32 * q : 32 * q + 8, 2560:3200],
-                        in_=s32[8, 4 * q : 4 * q + 4, :].rearrange("r (h c) -> h r c", h=2),
-                    )
-
         make_identity(nc, ident32[:])
-        load_scales(0)
         make_identity(nc, ident16[:])
-        load_scales(1)
-        load_scales(2)
+        p_two = p32[:, 0:2560].rearrange("p (s c) -> p s c", s=2)
+        for q in range(4):
+            for r in range(4):
+                nc.gpsimd.dma_start(
+                    out=p_two[32 * q + r : 32 * q + 16 : 4, :, :],
+                    in_=s32[0:8, 4 * q + r, :].rearrange("(s j) c -> j s c", j=4),
+                )
+        for q in range(4):
+            nc.gpsimd.dma_start(
+                out=p32[32 * q : 32 * q + 8, 2560:3200],
+                in_=s32[8, 4 * q : 4 * q + 4, :].rearrange("r (h c) -> h r c", h=2),
+            )
         nc.scalar.activation(out=warm[:], in_=ident32[:, 0:1], func=ACT.Sigmoid)
 
         nc.sync.dma_start(out=x_sb[:], in_=x)

@@ -25,6 +25,7 @@ R1_COL0 = 1024
 R1_BANKS = 8
 R2_BANKS = 2
 W_BUFS = 6
+QUARTER = N_OUT0 // 4
 
 INV0 = 1.0 / math.sqrt(MUL0)
 INV1 = 1.0 / math.sqrt(MUL1)
@@ -36,7 +37,7 @@ FLOPS = 2 * P * MUL0 * N_OUT0 + 2 * P * (DIM1 * MUL1 * MUL1 + DIM2 * MUL2 * MUL2
 def tile_equivariantmlpblock_w_kernel(tc, x, W0_words, W0_scales, W1, W2, out):
     nc = tc.nc
     w32 = W0_words.rearrange("g p n t -> g p (n t)").bitcast(I32)
-    s32 = W0_scales.bitcast(F32)
+    s32 = W0_scales.bitcast(I32)
 
     with ExitStack() as ctx:
         ctx.enter_context(tc.manual_schedule())
@@ -48,7 +49,7 @@ def tile_equivariantmlpblock_w_kernel(tc, x, W0_words, W0_scales, W1, W2, out):
             return psum.tile(shape, dtype, name=name, tag="bank%d" % bank)
 
         x_sb = keep.tile([P, D_ALL], BF16, name="x_sb", align_bytes=64)
-        planes = keep.tile([P, 2 * N_OUT0 + N_OUT0 // 2], U8, name="planes", align_bytes=64)
+        planes = keep.tile([P, 2 * N_OUT0 + QUARTER], U8, name="planes", align_bytes=64)
         ident32 = keep.tile([P, P], F32, name="ident32")
         ident16 = keep.tile([P, P], BF16, name="ident16")
         w1_sb = keep.tile([P, 3, MUL1], BF16, name="w1_sb")
@@ -66,28 +67,25 @@ def tile_equivariantmlpblock_w_kernel(tc, x, W0_words, W0_scales, W1, W2, out):
         ]
         r2_first = (0, 3, 6, 8)
 
-        p32 = planes[:].bitcast(F32)
-        for slot in range(3):
-            nc.vector.memset(planes[:, N_OUT0 * slot : min(N_OUT0 * (slot + 1), planes.shape[1])].bitcast(I32), 0)
-
+        nc.vector.memset(planes[:].bitcast(I32), 0)
         make_identity(nc, ident32[:])
         make_identity(nc, ident16[:])
-        p_two = p32[:, 0:2560].rearrange("p (s c) -> p s c", s=2)
-        for q in range(4):
-            for r in range(4):
-                nc.gpsimd.dma_start(
-                    out=p_two[32 * q + r : 32 * q + 16 : 4, :, :],
-                    in_=s32[0:8, 4 * q + r, :].rearrange("(s j) c -> j s c", j=4),
-                )
-        for q in range(4):
-            nc.gpsimd.dma_start(
-                out=p32[32 * q : 32 * q + 8, 2560:3200],
-                in_=s32[8, 4 * q : 4 * q + 4, :].rearrange("r (h c) -> h r c", h=2),
-            )
         nc.scalar.activation(out=warm[:], in_=ident32[:, 0:1], func=ACT.Sigmoid)
 
         nc.sync.dma_start(out=x_sb[:], in_=x)
-        nc.sync.dma_start(out=w1_sb[:], in_=W1.rearrange("(c p) o -> p c o", p=P))
+        p32 = planes[:].bitcast(I32)
+        for slot in range(2):
+            for q in range(4):
+                nc.sync.dma_start(
+                    out=p32[32 * q : 32 * q + 16, 1280 * slot : 1280 * (slot + 1)],
+                    in_=s32[4 * slot : 4 * slot + 4, 4 * q : 4 * q + 4, :],
+                )
+        for q in range(4):
+            nc.sync.dma_start(
+                out=p32[32 * q : 32 * q + 16, 2560:2880],
+                in_=s32[8, 4 * q : 4 * q + 4, :].rearrange("r (j c) -> j r c", j=4),
+            )
+        nc.sync.dma_start(out=w1_sb[:], in_=W1.rearrange("(p c) o -> p c o", c=3))
         nc.sync.dma_start(out=w2_sb[:], in_=W2)
 
         def load_round1(g):
@@ -97,15 +95,14 @@ def tile_equivariantmlpblock_w_kernel(tc, x, W0_words, W0_scales, W1, W2, out):
 
         w_r1 = [load_round1(g) for g in range(W_BUFS)]
 
-        def w_scale(g, col):
+        def w_scale(g, col, n):
             if g < 8:
                 k = 4 * (g % 4)
                 base = N_OUT0 * (g // 4) + col
             else:
-                h = col // (N_OUT0 // 2)
-                k = 4 * h
-                base = 2 * N_OUT0 + col - h * (N_OUT0 // 2)
-            return planes[k:P, base : base + BANK]
+                k = 4 * (col // QUARTER)
+                base = 2 * N_OUT0 + col % QUARTER
+            return planes[k:P, base : base + n]
 
         x32 = x_sb[:, 0:MUL0].bitcast(F32)
         g32 = grouped[:].bitcast(F32)
@@ -148,7 +145,7 @@ def tile_equivariantmlpblock_w_kernel(tc, x, W0_words, W0_scales, W1, W2, out):
 
         vt_ps = [bank_tile([P, 8, P], BF16, 5 + i, "vt_ps%d" % i) for i in range(2)]
         vt_src = [
-            x_sb[:, V0 + 384 * c + m : V0 + 384 * (c + 1) : DIM1] for c in range(3) for m in range(DIM1)
+            x_sb[:, V0 + DIM1 * c + m : T0 : 3 * DIM1] for c in range(3) for m in range(DIM1)
         ] + [x_sb[:, T0 + m : D_ALL : DIM2] for m in range(DIM2)]
         for i, src in enumerate(vt_src):
             nc.tensor.transpose(vt_ps[i // 7][:, i % 7, :], src, ident16[:])
@@ -190,15 +187,18 @@ def tile_equivariantmlpblock_w_kernel(tc, x, W0_words, W0_scales, W1, W2, out):
                 nc.scalar.activation(out=dst, in_=src, func=ACT.Copy, scale=INV2)
 
         def mx_pass(acc, g, words, col):
-            nc.tensor.matmul_mx(
-                out=acc[:],
-                lhsT=x_codes[:, P * g : P * (g + 1)].bitcast(FP8X4),
-                lhsT_scale=x_scales[:, P * g : P * (g + 1)],
-                rhs=words.bitcast(FP8X4),
-                rhs_scale=w_scale(g, col),
-                start=(g == 0),
-                stop=(g == GROUPS - 1),
-            )
+            split = g == 8 and col // QUARTER != (col + BANK - 1) // QUARTER
+            n = BANK // 2 if split else BANK
+            for lo in range(0, BANK, n):
+                nc.tensor.matmul_mx(
+                    out=acc[:, lo : lo + n],
+                    lhsT=x_codes[:, P * g : P * (g + 1)].bitcast(FP8X4),
+                    lhsT_scale=x_scales[:, P * g : P * (g + 1)],
+                    rhs=words[:, lo : lo + n].bitcast(FP8X4),
+                    rhs_scale=w_scale(g, col + lo, n),
+                    start=(g == 0),
+                    stop=(g == GROUPS - 1 and lo + n == BANK),
+                )
 
         def leaky(acc, col):
             dst = out_sb[:, col : col + BANK]
@@ -240,5 +240,5 @@ def tile_equivariantmlpblock_w_kernel(tc, x, W0_words, W0_scales, W1, W2, out):
         for b in range(R2_BANKS):
             leaky(acc2[b], BANK * b)
 
-        for lo, hi in ((1024, 2560), (2560, V0), (V0, D_ALL), (0, 1024)):
+        for lo, hi in ((1024, 2560), (2560, V0), (V0, D_ALL), (0, 512), (512, 1024)):
             nc.sync.dma_start(out=out[:, lo:hi], in_=out_sb[:, lo:hi])

from contextlib import ExitStack
import math

import concourse.mybir as mybir
from concourse.masks import make_identity

F32 = mybir.dt.float32
BF16 = mybir.dt.bfloat16
I32 = mybir.dt.int32
U32 = mybir.dt.uint32
U8 = mybir.dt.uint8
FP8X4 = mybir.dt.float8_e4m3fn_x4
ACT = mybir.ActivationFunctionType
ALU = mybir.AluOpType

P = 128
MUL0, MUL1, MUL2, DIM1, DIM2 = 4608, 384, 128, 3, 5
N_OUT0 = MUL0 + MUL1 + MUL2
GROUPS = MUL0 // 512
V0 = MUL0
T0 = MUL0 + MUL1 * DIM1
D_ALL = T0 + MUL2 * DIM2
BANK = 512
R1_COL0 = 1024
R1_BANKS = 8
R2_BANKS = 2
W_BUFS = 6
QUARTER = N_OUT0 // 4

INV0 = 1.0 / math.sqrt(MUL0)
INV1 = 1.0 / math.sqrt(MUL1)
INV2 = 1.0 / math.sqrt(MUL2)

FLOPS = 2 * P * MUL0 * N_OUT0 + 2 * P * (DIM1 * MUL1 * MUL1 + DIM2 * MUL2 * MUL2)


def tile_equivariantmlpblock_w_kernel(tc, x, W0_words, W0_scales, W1, W2, out):
    nc = tc.nc
    w32 = W0_words.rearrange("g p n t -> g p (n t)").bitcast(I32)
    s32 = W0_scales.bitcast(I32)

    with ExitStack() as ctx:
        ctx.enter_context(tc.manual_schedule())
        keep = ctx.enter_context(tc.tile_pool(name="keep", bufs=1))
        wpool = ctx.enter_context(tc.tile_pool(name="wstream", bufs=W_BUFS))
        psum = ctx.enter_context(tc.psum_pool(name="psum", bufs=1))

        def bank_tile(shape, dtype, bank, name):
            return psum.tile(shape, dtype, name=name, tag="bank%d" % bank)

        x_sb = keep.tile([P, D_ALL], BF16, name="x_sb", align_bytes=64)
        planes = keep.tile([P, 2 * N_OUT0 + QUARTER], U8, name="planes", align_bytes=64)
        ident32 = keep.tile([P, P], F32, name="ident32")
        ident16 = keep.tile([P, P], BF16, name="ident16")
        w1_sb = keep.tile([P, 3, MUL1], BF16, name="w1_sb")
        w2_sb = keep.tile([P, MUL2], BF16, name="w2_sb")
        grouped = keep.tile([P, GROUPS * 512], BF16, name="grouped", align_bytes=64)
        x_codes = keep.tile([P, GROUPS * P], U32, name="x_codes", align_bytes=64)
        x_scales = keep.tile([P, GROUPS * P], U8, name="x_scales", align_bytes=64)
        vt_sb = keep.tile([P, 14, P], BF16, name="vt_sb")
        out_sb = keep.tile([P, D_ALL], F32, name="out_sb")
        gates = keep.tile([P, BANK], F32, name="gates")
        warm = keep.tile([P, 1], F32, name="warm")
        w_r2 = [
            keep.tile([P, n, R2_BANKS * BANK], U32, name="w_r2_%d" % i, align_bytes=64)
            for i, n in enumerate((3, 3, 2, 1))
        ]
        r2_first = (0, 3, 6, 8)

        nc.vector.memset(planes[:].bitcast(I32), 0)
        make_identity(nc, ident32[:])
        make_identity(nc, ident16[:])
        nc.scalar.activation(out=warm[:], in_=ident32[:, 0:1], func=ACT.Sigmoid)

        nc.sync.dma_start(out=x_sb[:], in_=x)
        p32 = planes[:].bitcast(I32)
        for slot in range(2):
            for q in range(4):
                nc.sync.dma_start(
                    out=p32[32 * q : 32 * q + 16, 1280 * slot : 1280 * (slot + 1)],
                    in_=s32[4 * slot : 4 * slot + 4, 4 * q : 4 * q + 4, :],
                )
        for q in range(4):
            nc.sync.dma_start(
                out=p32[32 * q : 32 * q + 16, 2560:2880],
                in_=s32[8, 4 * q : 4 * q + 4, :].rearrange("r (j c) -> j r c", j=4),
            )
        nc.sync.dma_start(out=w1_sb[:], in_=W1.rearrange("(p c) o -> p c o", c=3))
        nc.sync.dma_start(out=w2_sb[:], in_=W2)

        def load_round1(g):
            w = wpool.tile([P, R1_BANKS * BANK], U32, name="w_r1", tag="w_r1", align_bytes=64)
            nc.sync.dma_start(out=w[:].bitcast(I32), in_=w32[g, :, R1_COL0:N_OUT0])
            return w

        w_r1 = [load_round1(g) for g in range(W_BUFS)]

        def w_scale(g, col, n):
            if g < 8:
                k = 4 * (g % 4)
                base = N_OUT0 * (g // 4) + col
            else:
                k = 4 * (col // QUARTER)
                base = 2 * N_OUT0 + col % QUARTER
            return planes[k:P, base : base + n]

        x32 = x_sb[:, 0:MUL0].bitcast(F32)
        g32 = grouped[:].bitcast(F32)
        s_ps = [bank_tile([P, 4, P], F32, i, "s_ps%d" % i) for i in range(5)]
        for g in range(GROUPS):
            for u in range(2):
                nc.tensor.transpose(
                    s_ps[g // 2][:, 2 * (g % 2) + u, :],
                    x32[:, 256 * g + u : 256 * (g + 1) : 2],
                    ident32[:],
                )

        def regroup(i, on_vector):
            ng = 2 if i < 4 else 1
            src = s_ps[i][:, 0 : 2 * ng, :].rearrange("p (g u) r -> p g r u", u=2)
            dst = g32[:, 512 * i : 512 * i + 256 * ng].rearrange("p (g r u) -> p g r u", g=ng, u=2)
            if on_vector:
                nc.vector.tensor_copy(out=dst, in_=src)
            else:
                nc.scalar.copy(out=dst, in_=src)

        def quantise(i):
            ng = 2 if i < 4 else 1
            nc.vector.quantize_mx(
                out=x_codes[:, 256 * i : 256 * i + P * ng].bitcast(FP8X4),
                scales=x_scales[:, 256 * i : 256 * i + P * ng],
                in_=grouped[:, 1024 * i : 1024 * i + 512 * ng],
            )

        regroup(0, True)
        regroup(1, False)
        regroup(2, True)
        regroup(3, False)
        quantise(0)
        regroup(4, True)
        quantise(1)
        quantise(2)
        quantise(3)
        quantise(4)

        vt_ps = [bank_tile([P, 8, P], BF16, 5 + i, "vt_ps%d" % i) for i in range(2)]
        vt_src = [
            x_sb[:, V0 + DIM1 * c + m : T0 : 3 * DIM1] for c in range(3) for m in range(DIM1)
        ] + [x_sb[:, T0 + m : D_ALL : DIM2] for m in range(DIM2)]
        for i, src in enumerate(vt_src):
            nc.tensor.transpose(vt_ps[i // 7][:, i % 7, :], src, ident16[:])
        nc.scalar.copy(out=vt_sb[:, 0:7, :], in_=vt_ps[0][:, 0:7, :])
        nc.vector.tensor_copy(out=vt_sb[:, 7:14, :], in_=vt_ps[1][:, 0:7, :])

        for oc in range(3):
            v_ps = bank_tile([P, DIM1, P], F32, (7, 0, 1)[oc], "v_ps%d" % oc)
            for m in range(DIM1):
                for c in range(3):
                    nc.tensor.matmul(
                        out=v_ps[:, m, :],
                        lhsT=vt_sb[:, 3 * c + m, :],
                        rhs=w1_sb[:, c, P * oc : P * (oc + 1)],
                        start=(c == 0),
                        stop=(c == 2),
                    )
            dst = out_sb[:, V0 + 384 * oc : V0 + 384 * (oc + 1)].rearrange("p (o m) -> p o m", m=DIM1)
            src = v_ps[:].rearrange("p m o -> p o m")
            if oc == 1:
                nc.vector.tensor_scalar(out=dst, in0=src, scalar1=INV1, scalar2=None, op0=ALU.mult)
            else:
                nc.scalar.activation(out=dst, in_=src, func=ACT.Copy, scale=INV1)
        for oh in range(2):
            t_ps = bank_tile([P, DIM2, 64], F32, (2, 3)[oh], "t_ps%d" % oh)
            for m in range(DIM2):
                nc.tensor.matmul(
                    out=t_ps[:, m, :],
                    lhsT=vt_sb[:, 9 + m, :],
                    rhs=w2_sb[:, 64 * oh : 64 * (oh + 1)],
                    start=True,
                    stop=True,
                )
            dst = out_sb[:, T0 + 320 * oh : T0 + 320 * (oh + 1)].rearrange("p (o m) -> p o m", m=DIM2)
            src = t_ps[:].rearrange("p m o -> p o m")
            if oh == 0:
                nc.vector.tensor_scalar(out=dst, in0=src, scalar1=INV2, scalar2=None, op0=ALU.mult)
            else:
                nc.scalar.activation(out=dst, in_=src, func=ACT.Copy, scale=INV2)

        def mx_pass(acc, g, words, col):
            split = g == 8 and col // QUARTER != (col + BANK - 1) // QUARTER
            n = BANK // 2 if split else BANK
            for lo in range(0, BANK, n):
                nc.tensor.matmul_mx(
                    out=acc[:, lo : lo + n],
                    lhsT=x_codes[:, P * g : P * (g + 1)].bitcast(FP8X4),
                    lhsT_scale=x_scales[:, P * g : P * (g + 1)],
                    rhs=words[:, lo : lo + n].bitcast(FP8X4),
                    rhs_scale=w_scale(g, col + lo, n),
                    start=(g == 0),
                    stop=(g == GROUPS - 1 and lo + n == BANK),
                )

        def leaky(acc, col):
            dst = out_sb[:, col : col + BANK]
            nc.scalar.activation(out=dst, in_=acc[:], func=ACT.Copy, scale=INV0)
            nc.vector.scalar_tensor_tensor(out=dst, in0=dst, scalar=0.01, in1=dst, op0=ALU.mult, op1=ALU.max)

        acc1 = [bank_tile([P, BANK], F32, (4 + b) % 8, "acc1_%d" % b) for b in range(R1_BANKS)]
        for g in range(GROUPS):
            for b in range(R1_BANKS):
                mx_pass(acc1[b], g, w_r1[g][:, BANK * b : BANK * (b + 1)], R1_COL0 + BANK * b)
            if g + W_BUFS < GROUPS:
                w_r1.append(load_round1(g + W_BUFS))
            if g + W_BUFS == GROUPS - 1:
                for i, tile_r2 in enumerate(w_r2):
                    g0 = r2_first[i]
                    n = tile_r2.shape[1]
                    nc.sync.dma_start(
                        out=tile_r2[:].bitcast(I32),
                        in_=w32[g0 : g0 + n, :, 0:R1_COL0].rearrange("g p w -> p g w"),
                    )

        for b in range(R1_BANKS - 1):
            leaky(acc1[b], R1_COL0 + BANK * b)
        nc.scalar.activation(out=gates[:], in_=acc1[R1_BANKS - 1][:], func=ACT.Sigmoid, scale=INV0)
        gv = out_sb[:, V0:T0].rearrange("p (o m) -> p o m", m=DIM1)
        nc.vector.tensor_tensor(
            out=gv, in0=gv, in1=gates[:, 0:MUL1].unsqueeze(2).to_broadcast([P, MUL1, DIM1]), op=ALU.mult
        )
        gt = out_sb[:, T0:D_ALL].rearrange("p (o m) -> p o m", m=DIM2)
        nc.vector.tensor_tensor(
            out=gt, in0=gt, in1=gates[:, MUL1:BANK].unsqueeze(2).to_broadcast([P, MUL2, DIM2]), op=ALU.mult
        )

        acc2 = [bank_tile([P, BANK], F32, (4 + b) % 8, "acc2_%d" % b) for b in range(R2_BANKS)]
        for i, tile_r2 in enumerate(w_r2):
            for j in range(tile_r2.shape[1]):
                for b in range(R2_BANKS):
                    mx_pass(acc2[b], r2_first[i] + j, tile_r2[:, j, BANK * b : BANK * (b + 1)], BANK * b)
        for b in range(R2_BANKS):
            leaky(acc2[b], BANK * b)

        for lo, hi in ((1024, 2560), (2560, V0), (V0, D_ALL), (0, 512), (512, 1024)):
            nc.sync.dma_start(out=out[:, lo:hi], in_=out_sb[:, lo:hi])
